import numpy as np
import ml_dtypes

BF16 = ml_dtypes.bfloat16


def bf(x):
    return np.asarray(x, np.float32).astype(BF16)


def f32(x):
    return np.asarray(x, np.float32)


def f64(x):
    return np.asarray(x).astype(np.float64)


def striped(idx):
    return np.tile(idx.reshape(-1, 16).T, (8, 1))


D, E, E2, S, NB, H, N = 1024, 1024, 2048, 1024, 8, 512, 8192


def setup_inputs():
    x = f32(bf(np.random.standard_normal((D, S))))
    w2 = bf(np.random.standard_normal((D, E)) / np.sqrt(D))
    gamma2 = f32(1.0 + 0.1 * np.random.standard_normal((E, 1)))
    beta2 = f32(0.1 * np.random.standard_normal((E, 1)))
    w1 = bf(np.random.standard_normal((E2, D)) / np.sqrt(E2))
    gamma1 = f32(1.0 + 0.1 * np.random.standard_normal((D, 1)))
    beta1 = f32(0.1 * np.random.standard_normal((D, 1)))
    idx = np.concatenate([np.random.permutation(S)[:H] for _ in range(N // H)])
    return {"x": x, "w2": w2, "gamma2": gamma2, "beta2": beta2, "w1": w1, "gamma1": gamma1, "beta1": beta1, "offs": striped(idx)}


def reference(x, w2, gamma2, beta2, w1, gamma1, beta1, offs):
    idx = offs[:16].T.reshape(-1)
    y = f64(w2).T @ f64(x)
    h = np.maximum(y[:, idx] * f64(gamma2) + f64(beta2), 0.0)
    h3 = h.reshape(E, S, NB)
    mx = h3.max(axis=-1)
    mn = h3.sum(axis=-1) / NB
    return (f64(w1)[:E].T @ mx + f64(w1)[E:].T @ mn) * f64(gamma1) + f64(beta1)

@@ -1,0 +1,145 @@
+import concourse.mybir as mybir
+
+F32 = mybir.dt.float32
+BF16 = mybir.dt.bfloat16
+U16 = mybir.dt.uint16
+ALU = mybir.AluOpType
+ACT = mybir.ActivationFunctionType
+AXIS = mybir.AxisListType
+
+P = 128
+D = 1024
+E = 1024
+S = 1024
+NB = 8
+BLOCKS = 8
+BANK = 512
+PIECE = 1024
+CHUNK = 256
+UNIT = CHUNK * NB
+
+FLOPS = 2 * D * E * S + 2 * (2 * E) * D * S
+
+
+def tile_featureextraction_b_kernel(tc, x, w2, gamma2, beta2, w1, gamma1, beta1, offs, out):
+    nc = tc.nc
+
+    x_blocks = x.rearrange("(p k) s -> p k s", k=BLOCKS)
+    w2_blocks = w2.rearrange("(p k) e -> p k e", k=BLOCKS)
+    w1_halves = w1.rearrange("(half p a) o -> half p a o", half=2, a=BLOCKS)
+    out_blocks = out.rearrange("(p b) n -> p b n", b=BLOCKS)
+
+    with (
+        tc.tile_pool(name="held", bufs=1) as held,
+        tc.tile_pool(name="stage", bufs=BLOCKS) as stage,
+        tc.tile_pool(name="work", bufs=3) as work,
+        tc.tile_pool(name="pooled", bufs=2) as pooled,
+        tc.tile_pool(name="results", bufs=2) as results,
+        tc.psum_pool(name="y_banks", bufs=4) as y_banks,
+        tc.psum_pool(name="out_banks", bufs=3) as out_banks,
+    ):
+        offsets = held.tile([P, S * NB // 16], U16, name="offsets")
+        nc.sync.dma_start(offsets[:], offs)
+
+        def load_vector(vector, name):
+            column = held.tile([P, BLOCKS], F32, name=name)
+            nc.scalar.dma_start(column[:], vector.rearrange("(p a) one -> p (a one)", a=BLOCKS))
+            return column
+
+        g2 = load_vector(gamma2, "g2")
+        b2 = load_vector(beta2, "b2")
+
+        x_f32 = []
+        w2_sb = []
+        for k in range(BLOCKS):
+            x_f32.append(stage.tile([P, S], F32, name="x_f32"))
+            nc.sync.dma_start(x_f32[k][:], x_blocks[:, k, :])
+            w2_sb.append(held.tile([P, E], BF16, name=f"w2_sb{k}"))
+            nc.scalar.dma_start(w2_sb[k][:], w2_blocks[:, k, :])
+
+        w1_sb = []
+        for half in range(2):
+            w1_sb.append(held.tile([P, BLOCKS, D], BF16, name=f"w1_sb{half}"))
+            nc.sync.dma_start(w1_sb[half][:], w1_halves[half])
+        g1 = load_vector(gamma1, "g1")
+        b1 = load_vector(beta1, "b1")
+
+        ones = held.tile([P, PIECE], F32, name="ones")
+        nc.gpsimd.memset(ones[:], 1.0)
+        gain = []
+        for a in range(BLOCKS):
+            gain.append(held.tile([P, PIECE], F32, name=f"gain{a}"))
+            nc.gpsimd.tensor_scalar(gain[a][:], ones[:], g2[:, a : a + 1], 0.0, ALU.mult, ALU.add)
+
+        x_bf = []
+        for k in range(BLOCKS):
+            x_bf.append(held.tile([P, S], BF16, name=f"x_bf{k}"))
+            if k % 2 == 0:
+                nc.vector.tensor_copy(x_bf[k][:], x_f32[k][:])
+            else:
+                nc.scalar.copy(x_bf[k][:], x_f32[k][:])
+
+        y = [held.tile([P, S], F32, name=f"y{a}") for a in range(BLOCKS)]
+
+        def project_in(a):
+            for first in range(0, S, BANK):
+                bank = y_banks.tile([P, BANK], F32, name="y_bank")
+                for k in range(BLOCKS):
+                    nc.tensor.matmul(
+                        bank[:],
+                        w2_sb[k][:, a::BLOCKS],
+                        x_bf[k][:, first : first + BANK],
+                        start=(k == 0),
+                        stop=(k == BLOCKS - 1),
+                    )
+                nc.scalar.copy(y[a][:, first : first + BANK], bank[:])
+
+        def unit(c, a):
+            scaled = work.tile([P, UNIT], F32, name="scaled")
+            for first in range(0, UNIT, PIECE):
+                column = (c * UNIT + first) // 16
+                nc.vector.tensor_tensor(
+                    scaled[:, first : first + PIECE],
+                    y[a][:].indirect(offsets[:, column : column + PIECE // 16]),
+                    gain[a][:],
+                    ALU.mult,
+                )
+            h = work.tile([P, UNIT], F32, name="h")
+            nc.scalar.activation(h[:], scaled[:], ACT.Relu, bias=b2[:, a : a + 1], scale=1.0)
+            by_point = h[:].rearrange("p (n t) -> p n t", t=NB)
+
+            mx = pooled.tile([P, CHUNK], BF16, name=f"mx{a}")
+            with nc.allow_low_precision(reason="a maximum is one of its inputs: it is rounded once"):
+                nc.vector.tensor_reduce(mx[:], by_point, AXIS.X, ALU.max)
+            total = pooled.tile([P, CHUNK], F32, name="total")
+            nc.vector.tensor_reduce(total[:], by_point, AXIS.X, ALU.add)
+            mn = pooled.tile([P, CHUNK], BF16, name=f"mn{a}")
+            nc.scalar.mul(mn[:], total[:], 1.0 / NB)
+            return mx, mn
+
+        def project_out(c, pooled_units):
+            for b in range(BLOCKS):
+                bank = out_banks.tile([P, CHUNK], F32, name="out_bank")
+                for a in range(BLOCKS):
+                    for half in range(2):
+                        nc.tensor.matmul(
+                            bank[:],
+                            w1_sb[half][:, a, b::BLOCKS],
+                            pooled_units[a][half][:],
+                            start=(a == 0 and half == 0),
+                            stop=(a == BLOCKS - 1 and half == 1),
+                        )
+                result = results.tile([P, CHUNK], F32, name="result")
+                nc.scalar.activation(
+                    result[:], bank[:], ACT.Identity, bias=b1[:, b : b + 1], scale=g1[:, b : b + 1]
+                )
+                nc.sync.dma_start(out_blocks[:, b, c * CHUNK : (c + 1) * CHUNK], result[:])
+
+        project_in(0)
+        for c in range(S // CHUNK):
+            pooled_units = []
+            for a in range(BLOCKS):
+                if c == 0 and a + 1 < BLOCKS:
+                    project_in(a + 1)
+                pooled_units.append(unit(c, a))
+            project_out(c, pooled_units)

@@ -31,59 +31,47 @@ def tile_featureextraction_b_kernel(tc, x, w2, gamma2, beta2, w1, gamma1, beta1,
 
     with (
         tc.tile_pool(name="held", bufs=1) as held,
-        tc.tile_pool(name="stage", bufs=BLOCKS) as stage,
-        tc.tile_pool(name="work", bufs=3) as work,
-        tc.tile_pool(name="pooled", bufs=2) as pooled,
-        tc.tile_pool(name="results", bufs=2) as results,
-        tc.psum_pool(name="y_banks", bufs=4) as y_banks,
-        tc.psum_pool(name="out_banks", bufs=3) as out_banks,
+        tc.psum_pool(name="banks", bufs=BLOCKS) as banks,
     ):
         offsets = held.tile([P, S * NB // 16], U16, name="offsets")
-        nc.sync.dma_start(offsets[:], offs)
-
-        def load_vector(vector, name):
-            column = held.tile([P, BLOCKS], F32, name=name)
-            nc.scalar.dma_start(column[:], vector.rearrange("(p a) one -> p (a one)", a=BLOCKS))
-            return column
-
-        g2 = load_vector(gamma2, "g2")
-        b2 = load_vector(beta2, "b2")
-
-        x_f32 = []
-        w2_sb = []
-        for k in range(BLOCKS):
-            x_f32.append(stage.tile([P, S], F32, name="x_f32"))
-            nc.sync.dma_start(x_f32[k][:], x_blocks[:, k, :])
-            w2_sb.append(held.tile([P, E], BF16, name=f"w2_sb{k}"))
-            nc.scalar.dma_start(w2_sb[k][:], w2_blocks[:, k, :])
-
-        w1_sb = []
-        for half in range(2):
-            w1_sb.append(held.tile([P, BLOCKS, D], BF16, name=f"w1_sb{half}"))
-            nc.sync.dma_start(w1_sb[half][:], w1_halves[half])
-        g1 = load_vector(gamma1, "g1")
-        b1 = load_vector(beta1, "b1")
-
+        g2 = held.tile([P, BLOCKS], F32, name="g2")
+        b2 = held.tile([P, BLOCKS], F32, name="b2")
+        g1 = held.tile([P, BLOCKS], F32, name="g1")
+        b1 = held.tile([P, BLOCKS], F32, name="b1")
+        b2_eighth = held.tile([P, BLOCKS], F32, name="b2_eighth")
         ones = held.tile([P, PIECE], F32, name="ones")
-        nc.gpsimd.memset(ones[:], 1.0)
-        gain = []
-        for a in range(BLOCKS):
-            gain.append(held.tile([P, PIECE], F32, name=f"gain{a}"))
-            nc.gpsimd.tensor_scalar(gain[a][:], ones[:], g2[:, a : a + 1], 0.0, ALU.mult, ALU.add)
-
-        x_bf = []
-        for k in range(BLOCKS):
-            x_bf.append(held.tile([P, S], BF16, name=f"x_bf{k}"))
-            if k % 2 == 0:
-                nc.vector.tensor_copy(x_bf[k][:], x_f32[k][:])
-            else:
-                nc.scalar.copy(x_bf[k][:], x_f32[k][:])
-
+        gain = [held.tile([P, PIECE], F32, name=f"gain{a}") for a in range(BLOCKS)]
+        w2_sb = [held.tile([P, E], BF16, name=f"w2_sb{k}") for k in range(BLOCKS)]
+        x_bf = [held.tile([P, S], BF16, name=f"x_bf{k}") for k in range(BLOCKS)]
+        w1_sb = [held.tile([P, BLOCKS, D], BF16, name=f"w1_sb{half}") for half in range(2)]
         y = [held.tile([P, S], F32, name=f"y{a}") for a in range(BLOCKS)]
 
-        def project_in(a):
+        def load_vector(column, vector):
+            nc.scalar.dma_start(column[:], vector.rearrange("(p a) one -> p (a one)", a=BLOCKS))
+
+        nc.sync.dma_start(offsets[:], offs)
+        load_vector(g2, gamma2)
+        load_vector(b2, beta2)
+        with tc.tile_pool(name="stage", bufs=BLOCKS) as stage:
+            x_f32 = [stage.tile([P, S], F32, name="x_f32") for k in range(BLOCKS)]
+            for k in range(BLOCKS):
+                nc.sync.dma_start(x_f32[k][:], x_blocks[:, k, :])
+                nc.scalar.dma_start(w2_sb[k][:], w2_blocks[:, k, :])
+            for half in range(2):
+                nc.sync.dma_start(w1_sb[half][:], w1_halves[half])
+            load_vector(g1, gamma1)
+            load_vector(b1, beta1)
+            for k in range(BLOCKS):
+                nc.vector.tensor_copy(x_bf[k][:], x_f32[k][:])
+
+        nc.gpsimd.memset(ones[:], 1.0)
+        for a in range(BLOCKS):
+            nc.gpsimd.tensor_scalar(gain[a][:], ones[:], g2[:, a : a + 1], 0.0, ALU.mult, ALU.add)
+        nc.gpsimd.tensor_scalar(b2_eighth[:], b2[:], 1.0 / NB, 0.0, ALU.mult, ALU.add)
+
+        for a in range(BLOCKS):
             for first in range(0, S, BANK):
-                bank = y_banks.tile([P, BANK], F32, name="y_bank")
+                bank = banks.tile([P, BANK], F32, name="bank")
                 for k in range(BLOCKS):
                     nc.tensor.matmul(
                         bank[:],
@@ -94,52 +82,65 @@ def tile_featureextraction_b_kernel(tc, x, w2, gamma2, beta2, w1, gamma1, beta1,
                     )
                 nc.scalar.copy(y[a][:, first : first + BANK], bank[:])
 
-        def unit(c, a):
-            scaled = work.tile([P, UNIT], F32, name="scaled")
-            for first in range(0, UNIT, PIECE):
-                column = (c * UNIT + first) // 16
-                nc.vector.tensor_tensor(
-                    scaled[:, first : first + PIECE],
-                    y[a][:].indirect(offsets[:, column : column + PIECE // 16]),
-                    gain[a][:],
-                    ALU.mult,
-                )
-            h = work.tile([P, UNIT], F32, name="h")
-            nc.scalar.activation(h[:], scaled[:], ACT.Relu, bias=b2[:, a : a + 1], scale=1.0)
-            by_point = h[:].rearrange("p (n t) -> p n t", t=NB)
-
-            mx = pooled.tile([P, CHUNK], BF16, name=f"mx{a}")
-            with nc.allow_low_precision(reason="a maximum is one of its inputs: it is rounded once"):
-                nc.vector.tensor_reduce(mx[:], by_point, AXIS.X, ALU.max)
-            total = pooled.tile([P, CHUNK], F32, name="total")
-            nc.vector.tensor_reduce(total[:], by_point, AXIS.X, ALU.add)
-            mn = pooled.tile([P, CHUNK], BF16, name=f"mn{a}")
-            nc.scalar.mul(mn[:], total[:], 1.0 / NB)
-            return mx, mn
-
-        def project_out(c, pooled_units):
-            for b in range(BLOCKS):
-                bank = out_banks.tile([P, CHUNK], F32, name="out_bank")
+        with (
+            tc.tile_pool(name="work", bufs=3) as work,
+            tc.tile_pool(name="pooled", bufs=BLOCKS) as pooled,
+            tc.tile_pool(name="results", bufs=3) as results,
+        ):
+            for c in range(S // CHUNK):
+                out_bank = [banks.tile([P, BANK], F32, name="bank") for b in range(BLOCKS)]
                 for a in range(BLOCKS):
-                    for half in range(2):
-                        nc.tensor.matmul(
-                            bank[:],
-                            w1_sb[half][:, a, b::BLOCKS],
-                            pooled_units[a][half][:],
-                            start=(a == 0 and half == 0),
-                            stop=(a == BLOCKS - 1 and half == 1),
+                    scaled = work.tile([P, UNIT], F32, name="scaled")
+                    for first in range(0, UNIT, PIECE):
+                        column = (c * UNIT + first) // 16
+                        nc.vector.tensor_tensor(
+                            scaled[:, first : first + PIECE],
+                            y[a][:].indirect(offsets[:, column : column + PIECE // 16]),
+                            gain[a][:],
+                            ALU.mult,
                         )
-                result = results.tile([P, CHUNK], F32, name="result")
-                nc.scalar.activation(
-                    result[:], bank[:], ACT.Identity, bias=b1[:, b : b + 1], scale=g1[:, b : b + 1]
-                )
-                nc.sync.dma_start(out_blocks[:, b, c * CHUNK : (c + 1) * CHUNK], result[:])
 
-        project_in(0)
-        for c in range(S // CHUNK):
-            pooled_units = []
-            for a in range(BLOCKS):
-                if c == 0 and a + 1 < BLOCKS:
-                    project_in(a + 1)
-                pooled_units.append(unit(c, a))
-            project_out(c, pooled_units)
+                    h_eighth = work.tile([P, CHUNK, NB], F32, name="h_eighth")
+                    nc.scalar.activation(
+                        h_eighth[:].rearrange("p n t -> p (n t)"),
+                        scaled[:],
+                        ACT.Relu,
+                        bias=b2_eighth[:, a : a + 1],
+                        scale=1.0 / NB,
+                    )
+                    h_bf = work.tile([P, CHUNK, NB], BF16, name="h_bf")
+                    nc.scalar.activation(
+                        h_bf[:].rearrange("p n t -> p (n t)"), scaled[:], ACT.Relu, bias=b2[:, a : a + 1], scale=1.0
+                    )
+
+                    mn = pooled.tile([P, CHUNK], BF16, name="mn")
+                    with nc.allow_low_precision(reason="summed in float32, rounded once on the way out"):
+                        nc.vector.tensor_reduce(mn[:], h_eighth[:], AXIS.X, ALU.add)
+
+                    best4 = work.tile([P, CHUNK, 4], BF16, name="best4")
+                    nc.vector.tensor_tensor(best4[:], h_bf[:, :, 0:4], h_bf[:, :, 4:8], ALU.max)
+                    best2 = work.tile([P, CHUNK, 2], BF16, name="best2")
+                    nc.vector.tensor_tensor(best2[:], best4[:, :, 0:2], best4[:, :, 2:4], ALU.max)
+                    mx = pooled.tile([P, CHUNK], BF16, name="mx")
+                    nc.vector.tensor_tensor(mx[:], best2[:, :, 0], best2[:, :, 1], ALU.max)
+
+                    for half, moving in ((1, mn), (0, mx)):
+                        for b in range(BLOCKS):
+                            nc.tensor.matmul(
+                                out_bank[b][:, :CHUNK],
+                                w1_sb[half][:, a, b::BLOCKS],
+                                moving[:],
+                                start=(a == 0 and half == 1),
+                                stop=(a == BLOCKS - 1 and half == 0),
+                            )
+
+                for b in range(BLOCKS):
+                    result = results.tile([P, CHUNK], F32, name="result")
+                    nc.scalar.activation(
+                        result[:],
+                        out_bank[b][:, :CHUNK],
+                        ACT.Identity,
+                        bias=b1[:, b : b + 1],
+                        scale=g1[:, b : b + 1],
+                    )
+                    nc.sync.dma_start(out_blocks[:, b, c * CHUNK : (c + 1) * CHUNK], result[:])

@@ -5,7 +5,6 @@ BF16 = mybir.dt.bfloat16
 U16 = mybir.dt.uint16
 ALU = mybir.AluOpType
 ACT = mybir.ActivationFunctionType
-AXIS = mybir.AxisListType
 
 P = 128
 D = 1024
@@ -113,9 +112,12 @@ def tile_featureextraction_b_kernel(tc, x, w2, gamma2, beta2, w1, gamma1, beta1,
                         h_bf[:].rearrange("p n t -> p (n t)"), scaled[:], ACT.Relu, bias=b2[:, a : a + 1], scale=1.0
                     )
 
+                    sum4 = work.tile([P, CHUNK, 4], F32, name="sum4")
+                    nc.gpsimd.tensor_tensor(sum4[:], h_eighth[:, :, 0:4], h_eighth[:, :, 4:8], ALU.add)
+                    sum2 = work.tile([P, CHUNK, 2], F32, name="sum2")
+                    nc.gpsimd.tensor_tensor(sum2[:], sum4[:, :, 0:2], sum4[:, :, 2:4], ALU.add)
                     mn = pooled.tile([P, CHUNK], BF16, name="mn")
-                    with nc.allow_low_precision(reason="summed in float32, rounded once on the way out"):
-                        nc.vector.tensor_reduce(mn[:], h_eighth[:], AXIS.X, ALU.add)
+                    nc.gpsimd.tensor_tensor(mn[:], sum2[:, :, 0], sum2[:, :, 1], ALU.add)
 
                     best4 = work.tile([P, CHUNK, 4], BF16, name="best4")
                     nc.vector.tensor_tensor(best4[:], h_bf[:, :, 0:4], h_bf[:, :, 4:8], ALU.max)

@@ -63,10 +63,10 @@ def tile_featureextraction_b_kernel(tc, x, w2, gamma2, beta2, w1, gamma1, beta1,
             for k in range(BLOCKS):
                 nc.vector.tensor_copy(x_bf[k][:], x_f32[k][:])
 
-        nc.gpsimd.memset(ones[:], 1.0)
+        nc.vector.memset(ones[:], 1.0)
         for a in range(BLOCKS):
-            nc.gpsimd.tensor_scalar(gain[a][:], ones[:], g2[:, a : a + 1], 0.0, ALU.mult, ALU.add)
-        nc.gpsimd.tensor_scalar(b2_eighth[:], b2[:], 1.0 / NB, 0.0, ALU.mult, ALU.add)
+            nc.vector.tensor_scalar_mul(gain[a][:], ones[:], g2[:, a : a + 1])
+        nc.vector.tensor_scalar_mul(b2_eighth[:], b2[:], 1.0 / NB)
 
         for a in range(BLOCKS):
             for first in range(0, S, BANK):
@@ -113,11 +113,11 @@ def tile_featureextraction_b_kernel(tc, x, w2, gamma2, beta2, w1, gamma1, beta1,
                     )
 
                     sum4 = work.tile([P, CHUNK, 4], F32, name="sum4")
-                    nc.gpsimd.tensor_tensor(sum4[:], h_eighth[:, :, 0:4], h_eighth[:, :, 4:8], ALU.add)
+                    nc.vector.tensor_tensor(sum4[:], h_eighth[:, :, 0:4], h_eighth[:, :, 4:8], ALU.add)
                     sum2 = work.tile([P, CHUNK, 2], F32, name="sum2")
-                    nc.gpsimd.tensor_tensor(sum2[:], sum4[:, :, 0:2], sum4[:, :, 2:4], ALU.add)
+                    nc.vector.tensor_tensor(sum2[:], sum4[:, :, 0:2], sum4[:, :, 2:4], ALU.add)
                     mn = pooled.tile([P, CHUNK], BF16, name="mn")
-                    nc.gpsimd.tensor_tensor(mn[:], sum2[:, :, 0], sum2[:, :, 1], ALU.add)
+                    nc.vector.tensor_tensor(mn[:], sum2[:, :, 0], sum2[:, :, 1], ALU.add)
 
                     best4 = work.tile([P, CHUNK, 4], BF16, name="best4")
                     nc.vector.tensor_tensor(best4[:], h_bf[:, :, 0:4], h_bf[:, :, 4:8], ALU.max)

@@ -1,4 +1,5 @@
 import concourse.mybir as mybir
+from concourse.masks import make_identity
 
 F32 = mybir.dt.float32
 BF16 = mybir.dt.bfloat16
@@ -16,6 +17,7 @@ BANK = 512
 PIECE = 1024
 CHUNK = 256
 UNIT = CHUNK * NB
+TENSOR_SUMS = 4
 
 FLOPS = 2 * D * E * S + 2 * (2 * E) * D * S
 
@@ -44,6 +46,8 @@ def tile_featureextraction_b_kernel(tc, x, w2, gamma2, beta2, w1, gamma1, beta1,
         x_bf = [held.tile([P, S], BF16, name=f"x_bf{k}") for k in range(BLOCKS)]
         w1_sb = [held.tile([P, BLOCKS, D], BF16, name=f"w1_sb{half}") for half in range(2)]
         y = [held.tile([P, S], F32, name=f"y{a}") for a in range(BLOCKS)]
+        identity = held.tile([P, P], F32, name="identity")
+        make_identity(nc, identity[:])
 
         def load_vector(column, vector):
             nc.scalar.dma_start(column[:], vector.rearrange("(p a) one -> p (a one)", a=BLOCKS))
@@ -86,63 +90,86 @@ def tile_featureextraction_b_kernel(tc, x, w2, gamma2, beta2, w1, gamma1, beta1,
             tc.tile_pool(name="pooled", bufs=BLOCKS) as pooled,
             tc.tile_pool(name="results", bufs=3) as results,
         ):
-            for c in range(S // CHUNK):
-                out_bank = [banks.tile([P, BANK], F32, name="bank") for b in range(BLOCKS)]
-                for a in range(BLOCKS):
-                    scaled = work.tile([P, UNIT], F32, name="scaled")
-                    for first in range(0, UNIT, PIECE):
-                        column = (c * UNIT + first) // 16
-                        nc.vector.tensor_tensor(
-                            scaled[:, first : first + PIECE],
-                            y[a][:].indirect(offsets[:, column : column + PIECE // 16]),
-                            gain[a][:],
-                            ALU.mult,
+
+            def pool_unit(c, a, tensor_sums):
+                scaled = work.tile([P, UNIT], F32, name="scaled")
+                for first in range(0, UNIT, PIECE):
+                    column = (c * UNIT + first) // 16
+                    nc.vector.tensor_tensor(
+                        scaled[:, first : first + PIECE],
+                        y[a][:].indirect(offsets[:, column : column + PIECE // 16]),
+                        gain[a][:],
+                        ALU.mult,
+                    )
+
+                h_eighth = work.tile([P, CHUNK, NB], F32, name="h_eighth")
+                nc.scalar.activation(
+                    h_eighth[:].rearrange("p n t -> p (n t)"),
+                    scaled[:],
+                    ACT.Relu,
+                    bias=b2_eighth[:, a : a + 1],
+                    scale=1.0 / NB,
+                )
+                h_bf = work.tile([P, CHUNK, NB], BF16, name="h_bf")
+                nc.scalar.activation(
+                    h_bf[:].rearrange("p n t -> p (n t)"), scaled[:], ACT.Relu, bias=b2[:, a : a + 1], scale=1.0
+                )
+
+                mn = pooled.tile([P, CHUNK], BF16, name="mn")
+                if tensor_sums:
+                    total = banks.tile([P, BANK], F32, name="bank")
+                    for t in range(NB):
+                        nc.tensor.matmul(
+                            total[:, :CHUNK], identity[:], h_eighth[:, :, t], start=(t == 0), stop=(t == NB - 1)
                         )
-
-                    h_eighth = work.tile([P, CHUNK, NB], F32, name="h_eighth")
-                    nc.scalar.activation(
-                        h_eighth[:].rearrange("p n t -> p (n t)"),
-                        scaled[:],
-                        ACT.Relu,
-                        bias=b2_eighth[:, a : a + 1],
-                        scale=1.0 / NB,
-                    )
-                    h_bf = work.tile([P, CHUNK, NB], BF16, name="h_bf")
-                    nc.scalar.activation(
-                        h_bf[:].rearrange("p n t -> p (n t)"), scaled[:], ACT.Relu, bias=b2[:, a : a + 1], scale=1.0
-                    )
-
+                    nc.scalar.copy(mn[:], total[:, :CHUNK])
+                else:
                     sum4 = work.tile([P, CHUNK, 4], F32, name="sum4")
                     nc.vector.tensor_tensor(sum4[:], h_eighth[:, :, 0:4], h_eighth[:, :, 4:8], ALU.add)
                     sum2 = work.tile([P, CHUNK, 2], F32, name="sum2")
                     nc.vector.tensor_tensor(sum2[:], sum4[:, :, 0:2], sum4[:, :, 2:4], ALU.add)
-                    mn = pooled.tile([P, CHUNK], BF16, name="mn")
                     nc.vector.tensor_tensor(mn[:], sum2[:, :, 0], sum2[:, :, 1], ALU.add)
 
-                    best4 = work.tile([P, CHUNK, 4], BF16, name="best4")
-                    nc.vector.tensor_tensor(best4[:], h_bf[:, :, 0:4], h_bf[:, :, 4:8], ALU.max)
-                    best2 = work.tile([P, CHUNK, 2], BF16, name="best2")
-                    nc.vector.tensor_tensor(best2[:], best4[:, :, 0:2], best4[:, :, 2:4], ALU.max)
-                    mx = pooled.tile([P, CHUNK], BF16, name="mx")
-                    nc.vector.tensor_tensor(mx[:], best2[:, :, 0], best2[:, :, 1], ALU.max)
+                best4 = work.tile([P, CHUNK, 4], BF16, name="best4")
+                nc.vector.tensor_tensor(best4[:], h_bf[:, :, 0:4], h_bf[:, :, 4:8], ALU.max)
+                best2 = work.tile([P, CHUNK, 2], BF16, name="best2")
+                nc.vector.tensor_tensor(best2[:], best4[:, :, 0:2], best4[:, :, 2:4], ALU.max)
+                mx = pooled.tile([P, CHUNK], BF16, name="mx")
+                nc.vector.tensor_tensor(mx[:], best2[:, :, 0], best2[:, :, 1], ALU.max)
+                return mx, mn
 
-                    for half, moving in ((1, mn), (0, mx)):
-                        for b in range(BLOCKS):
-                            nc.tensor.matmul(
-                                out_bank[b][:, :CHUNK],
-                                w1_sb[half][:, a, b::BLOCKS],
-                                moving[:],
-                                start=(a == 0 and half == 1),
-                                stop=(a == BLOCKS - 1 and half == 0),
-                            )
+            def project(out_bank, a, mx, mn):
+                for half, moving in ((1, mn), (0, mx)):
+                    for b in range(BLOCKS):
+                        nc.tensor.matmul(
+                            out_bank[b][:, :CHUNK],
+                            w1_sb[half][:, a, b::BLOCKS],
+                            moving[:],
+                            start=(a == 0 and half == 1),
+                            stop=(a == BLOCKS - 1 and half == 0),
+                        )
+
+            for c in range(S // CHUNK):
+                early = range(TENSOR_SUMS if c > 0 else 0)
+                early_pooled = [pool_unit(c, a, tensor_sums=True) for a in early]
+                out_bank = [banks.tile([P, BANK], F32, name="bank") for b in range(BLOCKS)]
+                for a in early:
+                    project(out_bank, a, *early_pooled[a])
+                for a in range(len(early), BLOCKS):
+                    project(out_bank, a, *pool_unit(c, a, tensor_sums=False))
 
                 for b in range(BLOCKS):
                     result = results.tile([P, CHUNK], F32, name="result")
-                    nc.scalar.activation(
-                        result[:],
-                        out_bank[b][:, :CHUNK],
-                        ACT.Identity,
-                        bias=b1[:, b : b + 1],
-                        scale=g1[:, b : b + 1],
-                    )
+                    if c == S // CHUNK - 1 and b % 2 == 1:
+                        nc.vector.tensor_scalar(
+                            result[:], out_bank[b][:, :CHUNK], g1[:, b : b + 1], b1[:, b : b + 1], ALU.mult, ALU.add
+                        )
+                    else:
+                        nc.scalar.activation(
+                            result[:],
+                            out_bank[b][:, :CHUNK],
+                            ACT.Identity,
+                            bias=b1[:, b : b + 1],
+                            scale=g1[:, b : b + 1],
+                        )
                     nc.sync.dma_start(out_blocks[:, b, c * CHUNK : (c + 1) * CHUNK], result[:])

@@ -13,6 +13,7 @@ E = 1024
 S = 1024
 NB = 8
 BLOCKS = 8
+GROUPS = 4
 BANK = 512
 PIECE = 1024
 CHUNK = 256
@@ -26,8 +27,8 @@ def tile_featureextraction_b_kernel(tc, x, w2, gamma2, beta2, w1, gamma1, beta1,
     nc = tc.nc
 
     x_blocks = x.rearrange("(p k) s -> p k s", k=BLOCKS)
-    w2_blocks = w2.rearrange("(p k) e -> p k e", k=BLOCKS)
-    w1_halves = w1.rearrange("(half p a) o -> half p a o", half=2, a=BLOCKS)
+    w2_groups = w2.rearrange("(p k) (g e) -> g p k e", k=BLOCKS, g=GROUPS)
+    w1_halves = w1.rearrange("(half g p j) o -> half p g (j o)", half=2, g=GROUPS, j=2)
     out_blocks = out.rearrange("(p b) n -> p b n", b=BLOCKS)
 
     with (
@@ -42,28 +43,31 @@ def tile_featureextraction_b_kernel(tc, x, w2, gamma2, beta2, w1, gamma1, beta1,
         b2_eighth = held.tile([P, BLOCKS], F32, name="b2_eighth")
         ones = held.tile([P, PIECE], F32, name="ones")
         gain = [held.tile([P, PIECE], F32, name=f"gain{a}") for a in range(BLOCKS)]
-        w2_sb = [held.tile([P, E], BF16, name=f"w2_sb{k}") for k in range(BLOCKS)]
+        w2_sb = [held.tile([P, BLOCKS, E // GROUPS], BF16, name=f"w2_sb{g}") for g in range(GROUPS)]
         x_bf = [held.tile([P, S], BF16, name=f"x_bf{k}") for k in range(BLOCKS)]
         w1_sb = [held.tile([P, BLOCKS, D], BF16, name=f"w1_sb{half}") for half in range(2)]
         y = [held.tile([P, S], F32, name=f"y{a}") for a in range(BLOCKS)]
         identity = held.tile([P, P], F32, name="identity")
         make_identity(nc, identity[:])
 
-        def load_vector(column, vector):
-            nc.scalar.dma_start(column[:], vector.rearrange("(p a) one -> p (a one)", a=BLOCKS))
-
         nc.sync.dma_start(offsets[:], offs)
-        load_vector(g2, gamma2)
-        load_vector(b2, beta2)
+        for column, vector in ((g2, gamma2), (b2, beta2)):
+            nc.scalar.dma_start(
+                column[:].rearrange("p (g j) -> p g j", j=2),
+                vector.rearrange("(g p j) one -> p g (j one)", g=GROUPS, j=2),
+            )
+        nc.sync.dma_start(w2_sb[0][:], w2_groups[0])
         with tc.tile_pool(name="stage", bufs=BLOCKS) as stage:
             x_f32 = [stage.tile([P, S], F32, name="x_f32") for k in range(BLOCKS)]
             for k in range(BLOCKS):
-                nc.sync.dma_start(x_f32[k][:], x_blocks[:, k, :])
-                nc.scalar.dma_start(w2_sb[k][:], w2_blocks[:, k, :])
+                queue = nc.sync if k % 2 == 0 else nc.scalar
+                queue.dma_start(x_f32[k][:], x_blocks[:, k, :])
+            for g in range(1, GROUPS):
+                nc.scalar.dma_start(w2_sb[g][:], w2_groups[g])
             for half in range(2):
-                nc.sync.dma_start(w1_sb[half][:], w1_halves[half])
-            load_vector(g1, gamma1)
-            load_vector(b1, beta1)
+                nc.sync.dma_start(w1_sb[half][:].rearrange("p (g j) o -> p g (j o)", j=2), w1_halves[half])
+            for column, vector in ((g1, gamma1), (b1, beta1)):
+                nc.scalar.dma_start(column[:], vector.rearrange("(p b) one -> p (b one)", b=BLOCKS))
             for k in range(BLOCKS):
                 nc.vector.tensor_copy(x_bf[k][:], x_f32[k][:])
 
@@ -78,7 +82,7 @@ def tile_featureextraction_b_kernel(tc, x, w2, gamma2, beta2, w1, gamma1, beta1,
                 for k in range(BLOCKS):
                     nc.tensor.matmul(
                         bank[:],
-                        w2_sb[k][:, a::BLOCKS],
+                        w2_sb[a // 2][:, k, a % 2 :: 2],
                         x_bf[k][:, first : first + BANK],
                         start=(k == 0),
                         stop=(k == BLOCKS - 1),
@@ -88,7 +92,7 @@ def tile_featureextraction_b_kernel(tc, x, w2, gamma2, beta2, w1, gamma1, beta1,
         with (
             tc.tile_pool(name="work", bufs=3) as work,
             tc.tile_pool(name="pooled", bufs=BLOCKS) as pooled,
-            tc.tile_pool(name="results", bufs=3) as results,
+            tc.tile_pool(name="results", bufs=BLOCKS) as results,
         ):
 
             def pool_unit(c, a, tensor_sums):

@@ -18,7 +18,7 @@ BANK = 512
 PIECE = 1024
 CHUNK = 256
 UNIT = CHUNK * NB
-TENSOR_SUMS = 4
+EARLY_UNITS = 5
 
 FLOPS = 2 * D * E * S + 2 * (2 * E) * D * S
 
@@ -154,8 +154,8 @@ def tile_featureextraction_b_kernel(tc, x, w2, gamma2, beta2, w1, gamma1, beta1,
                         )
 
             for c in range(S // CHUNK):
-                early = range(TENSOR_SUMS if c > 0 else 0)
-                early_pooled = [pool_unit(c, a, tensor_sums=True) for a in early]
+                early = range(EARLY_UNITS if c > 0 else 0)
+                early_pooled = [pool_unit(c, a, tensor_sums=(a % 2 == 0)) for a in early]
                 out_bank = [banks.tile([P, BANK], F32, name="bank") for b in range(BLOCKS)]
                 for a in early:
                     project(out_bank, a, *early_pooled[a])

@@ -13,12 +13,12 @@ E = 1024
 S = 1024
 NB = 8
 BLOCKS = 8
-GROUPS = 4
 BANK = 512
 PIECE = 1024
 CHUNK = 256
 UNIT = CHUNK * NB
 EARLY_UNITS = 5
+UNITS_BESIDE_Y = 4
 
 FLOPS = 2 * D * E * S + 2 * (2 * E) * D * S
 
@@ -27,8 +27,8 @@ def tile_featureextraction_b_kernel(tc, x, w2, gamma2, beta2, w1, gamma1, beta1,
     nc = tc.nc
 
     x_blocks = x.rearrange("(p k) s -> p k s", k=BLOCKS)
-    w2_groups = w2.rearrange("(p k) (g e) -> g p k e", k=BLOCKS, g=GROUPS)
-    w1_halves = w1.rearrange("(half g p j) o -> half p g (j o)", half=2, g=GROUPS, j=2)
+    w2_blocks = w2.rearrange("(p k) e -> p k e", k=BLOCKS)
+    w1_halves = w1.rearrange("(half p a) o -> half p a o", half=2, a=BLOCKS)
     out_blocks = out.rearrange("(p b) n -> p b n", b=BLOCKS)
 
     with (
@@ -43,31 +43,28 @@ def tile_featureextraction_b_kernel(tc, x, w2, gamma2, beta2, w1, gamma1, beta1,
         b2_eighth = held.tile([P, BLOCKS], F32, name="b2_eighth")
         ones = held.tile([P, PIECE], F32, name="ones")
         gain = [held.tile([P, PIECE], F32, name=f"gain{a}") for a in range(BLOCKS)]
-        w2_sb = [held.tile([P, BLOCKS, E // GROUPS], BF16, name=f"w2_sb{g}") for g in range(GROUPS)]
+        w2_sb = [held.tile([P, E], BF16, name=f"w2_sb{k}") for k in range(BLOCKS)]
         x_bf = [held.tile([P, S], BF16, name=f"x_bf{k}") for k in range(BLOCKS)]
         w1_sb = [held.tile([P, BLOCKS, D], BF16, name=f"w1_sb{half}") for half in range(2)]
         y = [held.tile([P, S], F32, name=f"y{a}") for a in range(BLOCKS)]
         identity = held.tile([P, P], F32, name="identity")
         make_identity(nc, identity[:])
 
+        def load_vector(column, vector):
+            nc.scalar.dma_start(column[:], vector.rearrange("(p a) one -> p (a one)", a=BLOCKS))
+
         nc.sync.dma_start(offsets[:], offs)
-        for column, vector in ((g2, gamma2), (b2, beta2)):
-            nc.scalar.dma_start(
-                column[:].rearrange("p (g j) -> p g j", j=2),
-                vector.rearrange("(g p j) one -> p g (j one)", g=GROUPS, j=2),
-            )
-        nc.sync.dma_start(w2_sb[0][:], w2_groups[0])
+        load_vector(g2, gamma2)
+        load_vector(b2, beta2)
         with tc.tile_pool(name="stage", bufs=BLOCKS) as stage:
             x_f32 = [stage.tile([P, S], F32, name="x_f32") for k in range(BLOCKS)]
             for k in range(BLOCKS):
-                queue = nc.sync if k % 2 == 0 else nc.scalar
-                queue.dma_start(x_f32[k][:], x_blocks[:, k, :])
-            for g in range(1, GROUPS):
-                nc.scalar.dma_start(w2_sb[g][:], w2_groups[g])
+                nc.sync.dma_start(x_f32[k][:], x_blocks[:, k, :])
+                nc.scalar.dma_start(w2_sb[k][:], w2_blocks[:, k, :])
             for half in range(2):
-                nc.sync.dma_start(w1_sb[half][:].rearrange("p (g j) o -> p g (j o)", j=2), w1_halves[half])
-            for column, vector in ((g1, gamma1), (b1, beta1)):
-                nc.scalar.dma_start(column[:], vector.rearrange("(p b) one -> p (b one)", b=BLOCKS))
+                nc.sync.dma_start(w1_sb[half][:], w1_halves[half])
+            load_vector(g1, gamma1)
+            load_vector(b1, beta1)
             for k in range(BLOCKS):
                 nc.vector.tensor_copy(x_bf[k][:], x_f32[k][:])
 
@@ -82,7 +79,7 @@ def tile_featureextraction_b_kernel(tc, x, w2, gamma2, beta2, w1, gamma1, beta1,
                 for k in range(BLOCKS):
                     nc.tensor.matmul(
                         bank[:],
-                        w2_sb[a // 2][:, k, a % 2 :: 2],
+                        w2_sb[k][:, a::BLOCKS],
                         x_bf[k][:, first : first + BANK],
                         start=(k == 0),
                         stop=(k == BLOCKS - 1),
@@ -154,8 +151,10 @@ def tile_featureextraction_b_kernel(tc, x, w2, gamma2, beta2, w1, gamma1, beta1,
                         )
 
             for c in range(S // CHUNK):
-                early = range(EARLY_UNITS if c > 0 else 0)
-                early_pooled = [pool_unit(c, a, tensor_sums=(a % 2 == 0)) for a in early]
+                early = range(EARLY_UNITS)
+                early_pooled = [
+                    pool_unit(c, a, tensor_sums=(a % 2 == 0 and c * BLOCKS + a >= UNITS_BESIDE_Y)) for a in early
+                ]
                 out_bank = [banks.tile([P, BANK], F32, name="bank") for b in range(BLOCKS)]
                 for a in early:
                     project(out_bank, a, *early_pooled[a])

@@ -17,7 +17,7 @@ BANK = 512
 PIECE = 1024
 CHUNK = 256
 UNIT = CHUNK * NB
-EARLY_UNITS = 5
+EARLY_UNITS = 4
 UNITS_BESIDE_Y = 4
 
 FLOPS = 2 * D * E * S + 2 * (2 * E) * D * S
@@ -151,9 +151,9 @@ def tile_featureextraction_b_kernel(tc, x, w2, gamma2, beta2, w1, gamma1, beta1,
                         )
 
             for c in range(S // CHUNK):
-                early = range(EARLY_UNITS)
+                early = range(EARLY_UNITS if c > 0 else UNITS_BESIDE_Y + 1)
                 early_pooled = [
-                    pool_unit(c, a, tensor_sums=(a % 2 == 0 and c * BLOCKS + a >= UNITS_BESIDE_Y)) for a in early
+                    pool_unit(c, a, tensor_sums=(a != 1 and c * BLOCKS + a >= UNITS_BESIDE_Y)) for a in early
                 ]
                 out_bank = [banks.tile([P, BANK], F32, name="bank") for b in range(BLOCKS)]
                 for a in early:

@@ -13,6 +13,7 @@ E = 1024
 S = 1024
 NB = 8
 BLOCKS = 8
+GROUPS = 4
 BANK = 512
 PIECE = 1024
 CHUNK = 256
@@ -27,8 +28,8 @@ def tile_featureextraction_b_kernel(tc, x, w2, gamma2, beta2, w1, gamma1, beta1,
     nc = tc.nc
 
     x_blocks = x.rearrange("(p k) s -> p k s", k=BLOCKS)
-    w2_blocks = w2.rearrange("(p k) e -> p k e", k=BLOCKS)
-    w1_halves = w1.rearrange("(half p a) o -> half p a o", half=2, a=BLOCKS)
+    w2_groups = w2.rearrange("(p k) (g e) -> g p k e", k=BLOCKS, g=GROUPS)
+    w1_halves = w1.rearrange("(half g p j) o -> half p g (j o)", half=2, g=GROUPS, j=2)
     out_blocks = out.rearrange("(p b) n -> p b n", b=BLOCKS)
 
     with (
@@ -43,48 +44,52 @@ def tile_featureextraction_b_kernel(tc, x, w2, gamma2, beta2, w1, gamma1, beta1,
         b2_eighth = held.tile([P, BLOCKS], F32, name="b2_eighth")
         ones = held.tile([P, PIECE], F32, name="ones")
         gain = [held.tile([P, PIECE], F32, name=f"gain{a}") for a in range(BLOCKS)]
-        w2_sb = [held.tile([P, E], BF16, name=f"w2_sb{k}") for k in range(BLOCKS)]
+        w2_sb = [held.tile([P, BLOCKS, E // GROUPS], BF16, name=f"w2_sb{g}") for g in range(GROUPS)]
         x_bf = [held.tile([P, S], BF16, name=f"x_bf{k}") for k in range(BLOCKS)]
         w1_sb = [held.tile([P, BLOCKS, D], BF16, name=f"w1_sb{half}") for half in range(2)]
         y = [held.tile([P, S], F32, name=f"y{a}") for a in range(BLOCKS)]
         identity = held.tile([P, P], F32, name="identity")
         make_identity(nc, identity[:])
 
-        def load_vector(column, vector):
-            nc.scalar.dma_start(column[:], vector.rearrange("(p a) one -> p (a one)", a=BLOCKS))
-
         nc.sync.dma_start(offsets[:], offs)
-        load_vector(g2, gamma2)
-        load_vector(b2, beta2)
+        for column, vector in ((g2, gamma2), (b2, beta2)):
+            nc.scalar.dma_start(
+                column[:].rearrange("p (g j) -> p g j", j=2),
+                vector.rearrange("(g p j) one -> p g (j one)", g=GROUPS, j=2),
+            )
+        nc.sync.dma_start(w2_sb[0][:], w2_groups[0])
         with tc.tile_pool(name="stage", bufs=BLOCKS) as stage:
             x_f32 = [stage.tile([P, S], F32, name="x_f32") for k in range(BLOCKS)]
             for k in range(BLOCKS):
                 nc.sync.dma_start(x_f32[k][:], x_blocks[:, k, :])
-                nc.scalar.dma_start(w2_sb[k][:], w2_blocks[:, k, :])
+            for g in range(1, GROUPS):
+                nc.sync.dma_start(w2_sb[g][:], w2_groups[g])
             for half in range(2):
-                nc.sync.dma_start(w1_sb[half][:], w1_halves[half])
-            load_vector(g1, gamma1)
-            load_vector(b1, beta1)
+                nc.sync.dma_start(w1_sb[half][:].rearrange("p (g j) o -> p g (j o)", j=2), w1_halves[half])
+            for column, vector in ((g1, gamma1), (b1, beta1)):
+                nc.scalar.dma_start(column[:], vector.rearrange("(p b) one -> p (b one)", b=BLOCKS))
             for k in range(BLOCKS):
                 nc.vector.tensor_copy(x_bf[k][:], x_f32[k][:])
 
         nc.vector.memset(ones[:], 1.0)
-        for a in range(BLOCKS):
-            nc.vector.tensor_scalar_mul(gain[a][:], ones[:], g2[:, a : a + 1])
         nc.vector.tensor_scalar_mul(b2_eighth[:], b2[:], 1.0 / NB)
 
         for a in range(BLOCKS):
+            nc.scalar.activation(gain[a][:], ones[:], ACT.Identity, scale=g2[:, a : a + 1])
             for first in range(0, S, BANK):
                 bank = banks.tile([P, BANK], F32, name="bank")
                 for k in range(BLOCKS):
                     nc.tensor.matmul(
                         bank[:],
-                        w2_sb[k][:, a::BLOCKS],
+                        w2_sb[a // 2][:, k, a % 2 :: 2],
                         x_bf[k][:, first : first + BANK],
                         start=(k == 0),
                         stop=(k == BLOCKS - 1),
                     )
-                nc.scalar.copy(y[a][:, first : first + BANK], bank[:])
+                if a == 0 and first > 0:
+                    nc.vector.tensor_copy(y[a][:, first : first + BANK], bank[:])
+                else:
+                    nc.scalar.copy(y[a][:, first : first + BANK], bank[:])
 
         with (
             tc.tile_pool(name="work", bufs=3) as work,

@@ -19,7 +19,7 @@ PIECE = 1024
 CHUNK = 256
 UNIT = CHUNK * NB
 EARLY_UNITS = 4
-UNITS_BESIDE_Y = 4
+UNITS_BESIDE_Y = 3
 
 FLOPS = 2 * D * E * S + 2 * (2 * E) * D * S
 
@@ -156,7 +156,7 @@ def tile_featureextraction_b_kernel(tc, x, w2, gamma2, beta2, w1, gamma1, beta1,
                         )
 
             for c in range(S // CHUNK):
-                early = range(EARLY_UNITS if c > 0 else UNITS_BESIDE_Y + 1)
+                early = range(EARLY_UNITS)
                 early_pooled = [
                     pool_unit(c, a, tensor_sums=(a != 1 and c * BLOCKS + a >= UNITS_BESIDE_Y)) for a in early
                 ]

@@ -18,8 +18,8 @@ BANK = 512
 PIECE = 1024
 CHUNK = 256
 UNIT = CHUNK * NB
-EARLY_UNITS = 4
-UNITS_BESIDE_Y = 3
+OUT_BANKS = BLOCKS * CHUNK // BANK
+FREE_BANKS = 8 - OUT_BANKS
 
 FLOPS = 2 * D * E * S + 2 * (2 * E) * D * S
 
@@ -34,7 +34,8 @@ def tile_featureextraction_b_kernel(tc, x, w2, gamma2, beta2, w1, gamma1, beta1,
 
     with (
         tc.tile_pool(name="held", bufs=1) as held,
-        tc.psum_pool(name="banks", bufs=BLOCKS) as banks,
+        tc.psum_pool(name="banks", bufs=FREE_BANKS) as banks,
+        tc.psum_pool(name="out_banks", bufs=OUT_BANKS) as out_banks,
     ):
         offsets = held.tile([P, S * NB // 16], U16, name="offsets")
         g2 = held.tile([P, BLOCKS], F32, name="g2")
@@ -50,6 +51,8 @@ def tile_featureextraction_b_kernel(tc, x, w2, gamma2, beta2, w1, gamma1, beta1,
         y = [held.tile([P, S], F32, name=f"y{a}") for a in range(BLOCKS)]
         identity = held.tile([P, P], F32, name="identity")
         make_identity(nc, identity[:])
+        identity_bf = held.tile([P, P], BF16, name="identity_bf")
+        make_identity(nc, identity_bf[:])
 
         nc.sync.dma_start(offsets[:], offs)
         for column, vector in ((g2, gamma2), (b2, beta2)):
@@ -73,9 +76,10 @@ def tile_featureextraction_b_kernel(tc, x, w2, gamma2, beta2, w1, gamma1, beta1,
 
         nc.vector.memset(ones[:], 1.0)
         nc.vector.tensor_scalar_mul(b2_eighth[:], b2[:], 1.0 / NB)
+        for a in range(BLOCKS):
+            nc.vector.tensor_scalar_mul(gain[a][:], ones[:], g2[:, a : a + 1])
 
         for a in range(BLOCKS):
-            nc.scalar.activation(gain[a][:], ones[:], ACT.Identity, scale=g2[:, a : a + 1])
             for first in range(0, S, BANK):
                 bank = banks.tile([P, BANK], F32, name="bank")
                 for k in range(BLOCKS):
@@ -97,7 +101,7 @@ def tile_featureextraction_b_kernel(tc, x, w2, gamma2, beta2, w1, gamma1, beta1,
             tc.tile_pool(name="results", bufs=BLOCKS) as results,
         ):
 
-            def pool_unit(c, a, tensor_sums):
+            def pool_unit(c, a):
                 scaled = work.tile([P, UNIT], F32, name="scaled")
                 for first in range(0, UNIT, PIECE):
                     column = (c * UNIT + first) // 16
@@ -121,20 +125,24 @@ def tile_featureextraction_b_kernel(tc, x, w2, gamma2, beta2, w1, gamma1, beta1,
                     h_bf[:].rearrange("p n t -> p (n t)"), scaled[:], ACT.Relu, bias=b2[:, a : a + 1], scale=1.0
                 )
 
-                mn = pooled.tile([P, CHUNK], BF16, name="mn")
-                if tensor_sums:
-                    total = banks.tile([P, BANK], F32, name="bank")
+                total = banks.tile([P, CHUNK], F32, name="total", tag="bank")
+                for first in range(0, CHUNK, P):
                     for t in range(NB):
                         nc.tensor.matmul(
-                            total[:, :CHUNK], identity[:], h_eighth[:, :, t], start=(t == 0), stop=(t == NB - 1)
+                            total[:, first : first + P],
+                            h_eighth[:, first : first + P, t],
+                            identity[:],
+                            is_transpose=True,
+                            start=(t == 0),
+                            stop=(t == NB - 1),
                         )
-                    nc.scalar.copy(mn[:], total[:, :CHUNK])
-                else:
-                    sum4 = work.tile([P, CHUNK, 4], F32, name="sum4")
-                    nc.vector.tensor_tensor(sum4[:], h_eighth[:, :, 0:4], h_eighth[:, :, 4:8], ALU.add)
-                    sum2 = work.tile([P, CHUNK, 2], F32, name="sum2")
-                    nc.vector.tensor_tensor(sum2[:], sum4[:, :, 0:2], sum4[:, :, 2:4], ALU.add)
-                    nc.vector.tensor_tensor(mn[:], sum2[:, :, 0], sum2[:, :, 1], ALU.add)
+                mn_turned = pooled.tile([P, CHUNK], BF16, name="mn_turned")
+                nc.scalar.copy(mn_turned[:], total[:])
+                back = banks.tile([P, CHUNK], BF16, name="back", tag="bank")
+                for first in range(0, CHUNK, P):
+                    nc.tensor.transpose(back[:, first : first + P], mn_turned[:, first : first + P], identity_bf[:])
+                mn = pooled.tile([P, CHUNK], BF16, name="mn")
+                nc.scalar.copy(mn[:], back[:])
 
                 best4 = work.tile([P, CHUNK, 4], BF16, name="best4")
                 nc.vector.tensor_tensor(best4[:], h_bf[:, :, 0:4], h_bf[:, :, 4:8], ALU.max)
@@ -147,35 +155,36 @@ def tile_featureextraction_b_kernel(tc, x, w2, gamma2, beta2, w1, gamma1, beta1,
             def project(out_bank, a, mx, mn):
                 for half, moving in ((1, mn), (0, mx)):
                     for b in range(BLOCKS):
+                        side = (b % 2) * CHUNK
                         nc.tensor.matmul(
-                            out_bank[b][:, :CHUNK],
+                            out_bank[b // 2][:, side : side + CHUNK],
                             w1_sb[half][:, a, b::BLOCKS],
                             moving[:],
-                            start=(a == 0 and half == 1),
-                            stop=(a == BLOCKS - 1 and half == 0),
+                            start=(a == 0 and half == 1 and b % 2 == 0),
+                            stop=(a == BLOCKS - 1 and half == 0 and b % 2 == 1),
                         )
 
             for c in range(S // CHUNK):
-                early = range(EARLY_UNITS)
-                early_pooled = [
-                    pool_unit(c, a, tensor_sums=(a != 1 and c * BLOCKS + a >= UNITS_BESIDE_Y)) for a in early
-                ]
-                out_bank = [banks.tile([P, BANK], F32, name="bank") for b in range(BLOCKS)]
-                for a in early:
-                    project(out_bank, a, *early_pooled[a])
-                for a in range(len(early), BLOCKS):
-                    project(out_bank, a, *pool_unit(c, a, tensor_sums=False))
+                out_bank = [out_banks.tile([P, BANK], F32, name="out_bank") for pair in range(OUT_BANKS)]
+                for a in range(BLOCKS):
+                    project(out_bank, a, *pool_unit(c, a))
 
                 for b in range(BLOCKS):
+                    side = (b % 2) * CHUNK
                     result = results.tile([P, CHUNK], F32, name="result")
-                    if c == S // CHUNK - 1 and b % 2 == 1:
+                    if c == S // CHUNK - 1 and (b // 2) % 2 == 1:
                         nc.vector.tensor_scalar(
-                            result[:], out_bank[b][:, :CHUNK], g1[:, b : b + 1], b1[:, b : b + 1], ALU.mult, ALU.add
+                            result[:],
+                            out_bank[b // 2][:, side : side + CHUNK],
+                            g1[:, b : b + 1],
+                            b1[:, b : b + 1],
+                            ALU.mult,
+                            ALU.add,
                         )
                     else:
                         nc.scalar.activation(
                             result[:],
-                            out_bank[b][:, :CHUNK],
+                            out_bank[b // 2][:, side : side + CHUNK],
                             ACT.Identity,
                             bias=b1[:, b : b + 1],
                             scale=g1[:, b : b + 1],

@@ -42,7 +42,6 @@ def tile_featureextraction_b_kernel(tc, x, w2, gamma2, beta2, w1, gamma1, beta1,
         b2 = held.tile([P, BLOCKS], F32, name="b2")
         g1 = held.tile([P, BLOCKS], F32, name="g1")
         b1 = held.tile([P, BLOCKS], F32, name="b1")
-        b2_eighth = held.tile([P, BLOCKS], F32, name="b2_eighth")
         ones = held.tile([P, PIECE], F32, name="ones")
         gain = [held.tile([P, PIECE], F32, name=f"gain{a}") for a in range(BLOCKS)]
         w2_sb = [held.tile([P, BLOCKS, E // GROUPS], BF16, name=f"w2_sb{g}") for g in range(GROUPS)]
@@ -75,7 +74,6 @@ def tile_featureextraction_b_kernel(tc, x, w2, gamma2, beta2, w1, gamma1, beta1,
                 nc.vector.tensor_copy(x_bf[k][:], x_f32[k][:])
 
         nc.vector.memset(ones[:], 1.0)
-        nc.vector.tensor_scalar_mul(b2_eighth[:], b2[:], 1.0 / NB)
         for a in range(BLOCKS):
             nc.vector.tensor_scalar_mul(gain[a][:], ones[:], g2[:, a : a + 1])
 
@@ -112,17 +110,9 @@ def tile_featureextraction_b_kernel(tc, x, w2, gamma2, beta2, w1, gamma1, beta1,
                         ALU.mult,
                     )
 
-                h_eighth = work.tile([P, CHUNK, NB], F32, name="h_eighth")
+                h = work.tile([P, CHUNK, NB], F32, name="h")
                 nc.scalar.activation(
-                    h_eighth[:].rearrange("p n t -> p (n t)"),
-                    scaled[:],
-                    ACT.Relu,
-                    bias=b2_eighth[:, a : a + 1],
-                    scale=1.0 / NB,
-                )
-                h_bf = work.tile([P, CHUNK, NB], BF16, name="h_bf")
-                nc.scalar.activation(
-                    h_bf[:].rearrange("p n t -> p (n t)"), scaled[:], ACT.Relu, bias=b2[:, a : a + 1], scale=1.0
+                    h[:].rearrange("p n t -> p (n t)"), scaled[:], ACT.Relu, bias=b2[:, a : a + 1], scale=1.0
                 )
 
                 total = banks.tile([P, CHUNK], F32, name="total", tag="bank")
@@ -130,14 +120,14 @@ def tile_featureextraction_b_kernel(tc, x, w2, gamma2, beta2, w1, gamma1, beta1,
                     for t in range(NB):
                         nc.tensor.matmul(
                             total[:, first : first + P],
-                            h_eighth[:, first : first + P, t],
+                            h[:, first : first + P, t],
                             identity[:],
                             is_transpose=True,
                             start=(t == 0),
                             stop=(t == NB - 1),
                         )
                 mn_turned = pooled.tile([P, CHUNK], BF16, name="mn_turned")
-                nc.scalar.copy(mn_turned[:], total[:])
+                nc.scalar.mul(mn_turned[:], total[:], 1.0 / NB)
                 back = banks.tile([P, CHUNK], BF16, name="back", tag="bank")
                 for first in range(0, CHUNK, P):
                     nc.tensor.transpose(back[:, first : first + P], mn_turned[:, first : first + P], identity_bf[:])
@@ -145,7 +135,7 @@ def tile_featureextraction_b_kernel(tc, x, w2, gamma2, beta2, w1, gamma1, beta1,
                 nc.scalar.copy(mn[:], back[:])
 
                 best4 = work.tile([P, CHUNK, 4], BF16, name="best4")
-                nc.vector.tensor_tensor(best4[:], h_bf[:, :, 0:4], h_bf[:, :, 4:8], ALU.max)
+                nc.vector.tensor_tensor(best4[:], h[:, :, 0:4], h[:, :, 4:8], ALU.max)
                 best2 = work.tile([P, CHUNK, 2], BF16, name="best2")
                 nc.vector.tensor_tensor(best2[:], best4[:, :, 0:2], best4[:, :, 2:4], ALU.max)
                 mx = pooled.tile([P, CHUNK], BF16, name="mx")

@@ -20,6 +20,9 @@ CHUNK = 256
 UNIT = CHUNK * NB
 OUT_BANKS = BLOCKS * CHUNK // BANK
 FREE_BANKS = 8 - OUT_BANKS
+UNITS = (S // CHUNK) * BLOCKS
+PASSES = 16
+VECTOR_SUMS = 4
 
 FLOPS = 2 * D * E * S + 2 * (2 * E) * D * S
 
@@ -42,6 +45,7 @@ def tile_featureextraction_b_kernel(tc, x, w2, gamma2, beta2, w1, gamma1, beta1,
         b2 = held.tile([P, BLOCKS], F32, name="b2")
         g1 = held.tile([P, BLOCKS], F32, name="g1")
         b1 = held.tile([P, BLOCKS], F32, name="b1")
+        b2_eighth = held.tile([P, BLOCKS], F32, name="b2_eighth")
         ones = held.tile([P, PIECE], F32, name="ones")
         gain = [held.tile([P, PIECE], F32, name=f"gain{a}") for a in range(BLOCKS)]
         w2_sb = [held.tile([P, BLOCKS, E // GROUPS], BF16, name=f"w2_sb{g}") for g in range(GROUPS)]
@@ -74,98 +78,132 @@ def tile_featureextraction_b_kernel(tc, x, w2, gamma2, beta2, w1, gamma1, beta1,
                 nc.vector.tensor_copy(x_bf[k][:], x_f32[k][:])
 
         nc.vector.memset(ones[:], 1.0)
+        nc.vector.tensor_scalar_mul(b2_eighth[:], b2[:], 1.0 / NB)
         for a in range(BLOCKS):
             nc.vector.tensor_scalar_mul(gain[a][:], ones[:], g2[:, a : a + 1])
 
-        for a in range(BLOCKS):
-            for first in range(0, S, BANK):
-                bank = banks.tile([P, BANK], F32, name="bank")
-                for k in range(BLOCKS):
-                    nc.tensor.matmul(
-                        bank[:],
-                        w2_sb[a // 2][:, k, a % 2 :: 2],
-                        x_bf[k][:, first : first + BANK],
-                        start=(k == 0),
-                        stop=(k == BLOCKS - 1),
-                    )
+        y_bank = {}
+
+        def y_pass(a, k):
+            first = (k // BLOCKS) * BANK
+            if k % BLOCKS == 0:
+                y_bank[a] = banks.tile([P, BANK], F32, name="bank")
+            nc.tensor.matmul(
+                y_bank[a][:],
+                w2_sb[a // 2][:, k % BLOCKS, a % 2 :: 2],
+                x_bf[k % BLOCKS][:, first : first + BANK],
+                start=(k % BLOCKS == 0),
+                stop=(k % BLOCKS == BLOCKS - 1),
+            )
+            if k % BLOCKS == BLOCKS - 1:
                 if a == 0 and first > 0:
-                    nc.vector.tensor_copy(y[a][:, first : first + BANK], bank[:])
+                    nc.vector.tensor_copy(y[a][:, first : first + BANK], y_bank[a][:])
                 else:
-                    nc.scalar.copy(y[a][:, first : first + BANK], bank[:])
+                    nc.scalar.copy(y[a][:, first : first + BANK], y_bank[a][:])
 
         with (
             tc.tile_pool(name="work", bufs=3) as work,
+            tc.tile_pool(name="partial_sums", bufs=2) as partial_sums,
             tc.tile_pool(name="pooled", bufs=BLOCKS) as pooled,
             tc.tile_pool(name="results", bufs=BLOCKS) as results,
         ):
+            scaled, h_eighth, h_bf, total, mn_turned, back, mn, mx, out_bank = {}, {}, {}, {}, {}, {}, {}, {}, {}
 
-            def pool_unit(c, a):
-                scaled = work.tile([P, UNIT], F32, name="scaled")
+            def gather(u):
+                c, a = divmod(u, BLOCKS)
+                scaled[u] = work.tile([P, UNIT], F32, name="scaled")
                 for first in range(0, UNIT, PIECE):
                     column = (c * UNIT + first) // 16
                     nc.vector.tensor_tensor(
-                        scaled[:, first : first + PIECE],
+                        scaled[u][:, first : first + PIECE],
                         y[a][:].indirect(offsets[:, column : column + PIECE // 16]),
                         gain[a][:],
                         ALU.mult,
                     )
 
-                h = work.tile([P, CHUNK, NB], F32, name="h")
+            def rectify(u):
+                a = u % BLOCKS
+                h_eighth[u] = work.tile([P, CHUNK, NB], F32, name="h_eighth")
                 nc.scalar.activation(
-                    h[:].rearrange("p n t -> p (n t)"), scaled[:], ACT.Relu, bias=b2[:, a : a + 1], scale=1.0
+                    h_eighth[u][:].rearrange("p n t -> p (n t)"),
+                    scaled[u][:],
+                    ACT.Relu,
+                    bias=b2_eighth[:, a : a + 1],
+                    scale=1.0 / NB,
+                )
+                h_bf[u] = work.tile([P, CHUNK, NB], BF16, name="h_bf")
+                nc.scalar.activation(
+                    h_bf[u][:].rearrange("p n t -> p (n t)"), scaled[u][:], ACT.Relu, bias=b2[:, a : a + 1], scale=1.0
                 )
 
-                total = banks.tile([P, CHUNK], F32, name="total", tag="bank")
-                for first in range(0, CHUNK, P):
-                    for t in range(NB):
-                        nc.tensor.matmul(
-                            total[:, first : first + P],
-                            h[:, first : first + P, t],
-                            identity[:],
-                            is_transpose=True,
-                            start=(t == 0),
-                            stop=(t == NB - 1),
-                        )
-                mn_turned = pooled.tile([P, CHUNK], BF16, name="mn_turned")
-                nc.scalar.mul(mn_turned[:], total[:], 1.0 / NB)
-                back = banks.tile([P, CHUNK], BF16, name="back", tag="bank")
-                for first in range(0, CHUNK, P):
-                    nc.tensor.transpose(back[:, first : first + P], mn_turned[:, first : first + P], identity_bf[:])
-                mn = pooled.tile([P, CHUNK], BF16, name="mn")
-                nc.scalar.copy(mn[:], back[:])
+            def sum_pass(u, k):
+                first, t = (k // NB) * P, k % NB
+                if k == 0:
+                    total[u] = banks.tile([P, CHUNK], F32, name="total", tag="bank")
+                nc.tensor.matmul(
+                    total[u][:, first : first + P],
+                    h_eighth[u][:, first : first + P, t],
+                    identity[:],
+                    is_transpose=True,
+                    start=(t == 0),
+                    stop=(t == NB - 1),
+                )
 
+            def maximum(u):
                 best4 = work.tile([P, CHUNK, 4], BF16, name="best4")
-                nc.vector.tensor_tensor(best4[:], h[:, :, 0:4], h[:, :, 4:8], ALU.max)
+                nc.vector.tensor_tensor(best4[:], h_bf[u][:, :, 0:4], h_bf[u][:, :, 4:8], ALU.max)
                 best2 = work.tile([P, CHUNK, 2], BF16, name="best2")
                 nc.vector.tensor_tensor(best2[:], best4[:, :, 0:2], best4[:, :, 2:4], ALU.max)
-                mx = pooled.tile([P, CHUNK], BF16, name="mx")
-                nc.vector.tensor_tensor(mx[:], best2[:, :, 0], best2[:, :, 1], ALU.max)
-                return mx, mn
+                mx[u] = pooled.tile([P, CHUNK], BF16, name="mx")
+                nc.vector.tensor_tensor(mx[u][:], best2[:, :, 0], best2[:, :, 1], ALU.max)
 
-            def project(out_bank, a, mx, mn):
-                for half, moving in ((1, mn), (0, mx)):
-                    for b in range(BLOCKS):
-                        side = (b % 2) * CHUNK
-                        nc.tensor.matmul(
-                            out_bank[b // 2][:, side : side + CHUNK],
-                            w1_sb[half][:, a, b::BLOCKS],
-                            moving[:],
-                            start=(a == 0 and half == 1 and b % 2 == 0),
-                            stop=(a == BLOCKS - 1 and half == 0 and b % 2 == 1),
-                        )
+            def vector_sum(u):
+                sum4 = partial_sums.tile([P, CHUNK, 4], F32, name="sum4")
+                nc.vector.tensor_tensor(sum4[:], h_eighth[u][:, :, 0:4], h_eighth[u][:, :, 4:8], ALU.add)
+                sum2 = partial_sums.tile([P, CHUNK, 2], F32, name="sum2")
+                nc.vector.tensor_tensor(sum2[:], sum4[:, :, 0:2], sum4[:, :, 2:4], ALU.add)
+                mn[u] = pooled.tile([P, CHUNK], BF16, name="mn")
+                nc.vector.tensor_tensor(mn[u][:], sum2[:, :, 0], sum2[:, :, 1], ALU.add)
 
-            for c in range(S // CHUNK):
-                out_bank = [out_banks.tile([P, BANK], F32, name="out_bank") for pair in range(OUT_BANKS)]
-                for a in range(BLOCKS):
-                    project(out_bank, a, *pool_unit(c, a))
+            def round_mean(u):
+                mn_turned[u] = work.tile([P, CHUNK], BF16, name="mn_turned")
+                nc.scalar.copy(mn_turned[u][:], total[u][:])
 
+            def turn_back(u):
+                back[u] = banks.tile([P, CHUNK], BF16, name="back", tag="bank")
+                for first in range(0, CHUNK, P):
+                    nc.tensor.transpose(
+                        back[u][:, first : first + P], mn_turned[u][:, first : first + P], identity_bf[:]
+                    )
+
+            def fetch_mean(u):
+                mn[u] = pooled.tile([P, CHUNK], BF16, name="mn")
+                nc.scalar.copy(mn[u][:], back[u][:])
+
+            def project_pass(u, k):
+                c, a = divmod(u, BLOCKS)
+                first_half, b = k < BLOCKS, k % BLOCKS
+                if a == 0 and k == 0:
+                    out_bank[c] = [out_banks.tile([P, BANK], F32, name="out_bank") for pair in range(OUT_BANKS)]
+                side = (b % 2) * CHUNK
+                nc.tensor.matmul(
+                    out_bank[c][b // 2][:, side : side + CHUNK],
+                    w1_sb[1 if first_half else 0][:, a, b::BLOCKS],
+                    (mn[u] if first_half else mx[u])[:],
+                    start=(a == 0 and first_half and b % 2 == 0),
+                    stop=(a == BLOCKS - 1 and not first_half and b % 2 == 1),
+                )
+                if a == BLOCKS - 1 and k == PASSES - 1:
+                    store(c)
+
+            def store(c):
                 for b in range(BLOCKS):
                     side = (b % 2) * CHUNK
                     result = results.tile([P, CHUNK], F32, name="result")
                     if c == S // CHUNK - 1 and (b // 2) % 2 == 1:
                         nc.vector.tensor_scalar(
                             result[:],
-                            out_bank[b // 2][:, side : side + CHUNK],
+                            out_bank[c][b // 2][:, side : side + CHUNK],
                             g1[:, b : b + 1],
                             b1[:, b : b + 1],
                             ALU.mult,
@@ -174,9 +212,35 @@ def tile_featureextraction_b_kernel(tc, x, w2, gamma2, beta2, w1, gamma1, beta1,
                     else:
                         nc.scalar.activation(
                             result[:],
-                            out_bank[b // 2][:, side : side + CHUNK],
+                            out_bank[c][b // 2][:, side : side + CHUNK],
                             ACT.Identity,
                             bias=b1[:, b : b + 1],
                             scale=g1[:, b : b + 1],
                         )
                     nc.sync.dma_start(out_blocks[:, b, c * CHUNK : (c + 1) * CHUNK], result[:])
+
+            Y_AHEAD = 2
+            SUM_LAG, PROJECT_LAG = 2, 6
+            stages = (
+                (fetch_mean, 5, VECTOR_SUMS, UNITS),
+                (turn_back, 4, VECTOR_SUMS, UNITS),
+                (round_mean, 3, VECTOR_SUMS, UNITS),
+                (vector_sum, SUM_LAG, 0, VECTOR_SUMS),
+                (maximum, 2, 0, UNITS),
+                (rectify, 1, 0, UNITS),
+                (gather, 0, 0, UNITS),
+            )
+            for a in range(Y_AHEAD):
+                for k in range(PASSES):
+                    y_pass(a, k)
+            for step in range(UNITS + PROJECT_LAG):
+                for k in range(PASSES):
+                    if step + Y_AHEAD < BLOCKS:
+                        y_pass(step + Y_AHEAD, k)
+                    if VECTOR_SUMS <= step - SUM_LAG < UNITS:
+                        sum_pass(step - SUM_LAG, k)
+                    if 0 <= step - PROJECT_LAG < UNITS:
+                        project_pass(step - PROJECT_LAG, k)
+                for run_stage, lag, first_unit, end_unit in stages:
+                    if first_unit <= step - lag < end_unit:
+                        run_stage(step - lag)

@@ -22,7 +22,7 @@ OUT_BANKS = BLOCKS * CHUNK // BANK
 FREE_BANKS = 8 - OUT_BANKS
 UNITS = (S // CHUNK) * BLOCKS
 PASSES = 16
-VECTOR_SUMS = 4
+VECTOR_SUMS = 2
 
 FLOPS = 2 * D * E * S + 2 * (2 * E) * D * S
 
@@ -188,8 +188,8 @@ def tile_featureextraction_b_kernel(tc, x, w2, gamma2, beta2, w1, gamma1, beta1,
                 side = (b % 2) * CHUNK
                 nc.tensor.matmul(
                     out_bank[c][b // 2][:, side : side + CHUNK],
-                    w1_sb[1 if first_half else 0][:, a, b::BLOCKS],
-                    (mn[u] if first_half else mx[u])[:],
+                    w1_sb[0 if first_half else 1][:, a, b::BLOCKS],
+                    (mx[u] if first_half else mn[u])[:],
                     start=(a == 0 and first_half and b % 2 == 0),
                     stop=(a == BLOCKS - 1 and not first_half and b % 2 == 1),
                 )
@@ -220,14 +220,14 @@ def tile_featureextraction_b_kernel(tc, x, w2, gamma2, beta2, w1, gamma1, beta1,
                     nc.sync.dma_start(out_blocks[:, b, c * CHUNK : (c + 1) * CHUNK], result[:])
 
             Y_AHEAD = 2
-            SUM_LAG, PROJECT_LAG = 2, 6
+            SUM_LAG, PROJECT_LAG = 2, 5
             stages = (
-                (fetch_mean, 5, VECTOR_SUMS, UNITS),
-                (turn_back, 4, VECTOR_SUMS, UNITS),
                 (round_mean, 3, VECTOR_SUMS, UNITS),
+                (turn_back, 3, VECTOR_SUMS, UNITS),
                 (vector_sum, SUM_LAG, 0, VECTOR_SUMS),
                 (maximum, 2, 0, UNITS),
                 (rectify, 1, 0, UNITS),
+                (fetch_mean, 4, VECTOR_SUMS, UNITS),
                 (gather, 0, 0, UNITS),
             )
             for a in range(Y_AHEAD):

@@ -237,8 +237,10 @@ def tile_featureextraction_b_kernel(tc, x, w2, gamma2, beta2, w1, gamma1, beta1,
                 for k in range(PASSES):
                     if step + Y_AHEAD < BLOCKS:
                         y_pass(step + Y_AHEAD, k)
+                for k in range(PASSES):
                     if VECTOR_SUMS <= step - SUM_LAG < UNITS:
                         sum_pass(step - SUM_LAG, k)
+                for k in range(PASSES):
                     if 0 <= step - PROJECT_LAG < UNITS:
                         project_pass(step - PROJECT_LAG, k)
                 for run_stage, lag, first_unit, end_unit in stages:

@@ -103,7 +103,8 @@ def tile_featureextraction_b_kernel(tc, x, w2, gamma2, beta2, w1, gamma1, beta1,
 
         with (
             tc.tile_pool(name="work", bufs=3) as work,
-            tc.tile_pool(name="partial_sums", bufs=2) as partial_sums,
+            tc.tile_pool(name="partial_sums", bufs=1) as partial_sums,
+            tc.tile_pool(name="pairs", bufs=2) as pairs,
             tc.tile_pool(name="pooled", bufs=BLOCKS) as pooled,
             tc.tile_pool(name="results", bufs=BLOCKS) as results,
         ):
@@ -131,9 +132,14 @@ def tile_featureextraction_b_kernel(tc, x, w2, gamma2, beta2, w1, gamma1, beta1,
                     bias=b2_eighth[:, a : a + 1],
                     scale=1.0 / NB,
                 )
-                h_bf[u] = work.tile([P, CHUNK, NB], BF16, name="h_bf")
+                if u % 2 == 0:
+                    h_bf[u // 2] = pairs.tile([P, 2 * CHUNK, NB], BF16, name="h_bf")
                 nc.scalar.activation(
-                    h_bf[u][:].rearrange("p n t -> p (n t)"), scaled[u][:], ACT.Relu, bias=b2[:, a : a + 1], scale=1.0
+                    h_bf[u // 2][:, (u % 2) * CHUNK : (u % 2 + 1) * CHUNK, :].rearrange("p n t -> p (n t)"),
+                    scaled[u][:],
+                    ACT.Relu,
+                    bias=b2[:, a : a + 1],
+                    scale=1.0,
                 )
 
             def sum_pass(u, k):
@@ -150,12 +156,13 @@ def tile_featureextraction_b_kernel(tc, x, w2, gamma2, beta2, w1, gamma1, beta1,
                 )
 
             def maximum(u):
-                best4 = work.tile([P, CHUNK, 4], BF16, name="best4")
-                nc.vector.tensor_tensor(best4[:], h_bf[u][:, :, 0:4], h_bf[u][:, :, 4:8], ALU.max)
-                best2 = work.tile([P, CHUNK, 2], BF16, name="best2")
+                pair = u // 2
+                best4 = pairs.tile([P, 2 * CHUNK, 4], BF16, name="best4")
+                nc.vector.tensor_tensor(best4[:], h_bf[pair][:, :, 0:4], h_bf[pair][:, :, 4:8], ALU.max)
+                best2 = pairs.tile([P, 2 * CHUNK, 2], BF16, name="best2")
                 nc.vector.tensor_tensor(best2[:], best4[:, :, 0:2], best4[:, :, 2:4], ALU.max)
-                mx[u] = pooled.tile([P, CHUNK], BF16, name="mx")
-                nc.vector.tensor_tensor(mx[u][:], best2[:, :, 0], best2[:, :, 1], ALU.max)
+                mx[pair] = pooled.tile([P, 2 * CHUNK], BF16, name="mx", bufs=BLOCKS // 2)
+                nc.vector.tensor_tensor(mx[pair][:], best2[:, :, 0], best2[:, :, 1], ALU.max)
 
             def vector_sum(u):
                 sum4 = partial_sums.tile([P, CHUNK, 4], F32, name="sum4")
@@ -189,7 +196,7 @@ def tile_featureextraction_b_kernel(tc, x, w2, gamma2, beta2, w1, gamma1, beta1,
                 nc.tensor.matmul(
                     out_bank[c][b // 2][:, side : side + CHUNK],
                     w1_sb[0 if first_half else 1][:, a, b::BLOCKS],
-                    (mx[u] if first_half else mn[u])[:],
+                    mx[u // 2][:, (u % 2) * CHUNK : (u % 2 + 1) * CHUNK] if first_half else mn[u][:],
                     start=(a == 0 and first_half and b % 2 == 0),
                     stop=(a == BLOCKS - 1 and not first_half and b % 2 == 1),
                 )
@@ -221,14 +228,18 @@ def tile_featureextraction_b_kernel(tc, x, w2, gamma2, beta2, w1, gamma1, beta1,
 
             Y_AHEAD = 2
             SUM_LAG, PROJECT_LAG = 2, 5
+            every_unit = range(UNITS)
+            odd_units = range(1, UNITS, 2)
+            vector_sums = [u for u in every_unit if u < VECTOR_SUMS or u == UNITS - 2]
+            tensor_sums = [u for u in every_unit if u not in vector_sums]
             stages = (
-                (round_mean, 3, VECTOR_SUMS, UNITS),
-                (turn_back, 3, VECTOR_SUMS, UNITS),
-                (vector_sum, SUM_LAG, 0, VECTOR_SUMS),
-                (maximum, 2, 0, UNITS),
-                (rectify, 1, 0, UNITS),
-                (fetch_mean, 4, VECTOR_SUMS, UNITS),
-                (gather, 0, 0, UNITS),
+                (round_mean, 3, tensor_sums),
+                (turn_back, 3, tensor_sums),
+                (vector_sum, SUM_LAG, vector_sums),
+                (maximum, 2, odd_units),
+                (rectify, 1, every_unit),
+                (fetch_mean, 4, tensor_sums),
+                (gather, 0, every_unit),
             )
             for a in range(Y_AHEAD):
                 for k in range(PASSES):
@@ -238,11 +249,11 @@ def tile_featureextraction_b_kernel(tc, x, w2, gamma2, beta2, w1, gamma1, beta1,
                     if step + Y_AHEAD < BLOCKS:
                         y_pass(step + Y_AHEAD, k)
                 for k in range(PASSES):
-                    if VECTOR_SUMS <= step - SUM_LAG < UNITS:
+                    if step - SUM_LAG in tensor_sums:
                         sum_pass(step - SUM_LAG, k)
                 for k in range(PASSES):
-                    if 0 <= step - PROJECT_LAG < UNITS:
+                    if step - PROJECT_LAG in every_unit:
                         project_pass(step - PROJECT_LAG, k)
-                for run_stage, lag, first_unit, end_unit in stages:
-                    if first_unit <= step - lag < end_unit:
+                for run_stage, lag, its_units in stages:
+                    if step - lag in its_units:
                         run_stage(step - lag)

@@ -22,7 +22,7 @@ OUT_BANKS = BLOCKS * CHUNK // BANK
 FREE_BANKS = 8 - OUT_BANKS
 UNITS = (S // CHUNK) * BLOCKS
 PASSES = 16
-VECTOR_SUMS = 2
+VECTOR_SUMS = 1
 
 FLOPS = 2 * D * E * S + 2 * (2 * E) * D * S
 

import concourse.mybir as mybir
from concourse.masks import make_identity

F32 = mybir.dt.float32
BF16 = mybir.dt.bfloat16
U16 = mybir.dt.uint16
ALU = mybir.AluOpType
ACT = mybir.ActivationFunctionType

P = 128
D = 1024
E = 1024
S = 1024
NB = 8
BLOCKS = 8
GROUPS = 4
BANK = 512
PIECE = 1024
CHUNK = 256
UNIT = CHUNK * NB
OUT_BANKS = BLOCKS * CHUNK // BANK
FREE_BANKS = 8 - OUT_BANKS
UNITS = (S // CHUNK) * BLOCKS
PASSES = 16
VECTOR_SUMS = 1

FLOPS = 2 * D * E * S + 2 * (2 * E) * D * S


def tile_featureextraction_b_kernel(tc, x, w2, gamma2, beta2, w1, gamma1, beta1, offs, out):
    nc = tc.nc

    x_blocks = x.rearrange("(p k) s -> p k s", k=BLOCKS)
    w2_groups = w2.rearrange("(p k) (g e) -> g p k e", k=BLOCKS, g=GROUPS)
    w1_halves = w1.rearrange("(half g p j) o -> half p g (j o)", half=2, g=GROUPS, j=2)
    out_blocks = out.rearrange("(p b) n -> p b n", b=BLOCKS)

    with (
        tc.tile_pool(name="held", bufs=1) as held,
        tc.psum_pool(name="banks", bufs=FREE_BANKS) as banks,
        tc.psum_pool(name="out_banks", bufs=OUT_BANKS) as out_banks,
    ):
        offsets = held.tile([P, S * NB // 16], U16, name="offsets")
        g2 = held.tile([P, BLOCKS], F32, name="g2")
        b2 = held.tile([P, BLOCKS], F32, name="b2")
        g1 = held.tile([P, BLOCKS], F32, name="g1")
        b1 = held.tile([P, BLOCKS], F32, name="b1")
        b2_eighth = held.tile([P, BLOCKS], F32, name="b2_eighth")
        ones = held.tile([P, PIECE], F32, name="ones")
        gain = [held.tile([P, PIECE], F32, name=f"gain{a}") for a in range(BLOCKS)]
        w2_sb = [held.tile([P, BLOCKS, E // GROUPS], BF16, name=f"w2_sb{g}") for g in range(GROUPS)]
        x_bf = [held.tile([P, S], BF16, name=f"x_bf{k}") for k in range(BLOCKS)]
        w1_sb = [held.tile([P, BLOCKS, D], BF16, name=f"w1_sb{half}") for half in range(2)]
        y = [held.tile([P, S], F32, name=f"y{a}") for a in range(BLOCKS)]
        identity = held.tile([P, P], F32, name="identity")
        make_identity(nc, identity[:])
        identity_bf = held.tile([P, P], BF16, name="identity_bf")
        make_identity(nc, identity_bf[:])

        nc.sync.dma_start(offsets[:], offs)
        for column, vector in ((g2, gamma2), (b2, beta2)):
            nc.scalar.dma_start(
                column[:].rearrange("p (g j) -> p g j", j=2),
                vector.rearrange("(g p j) one -> p g (j one)", g=GROUPS, j=2),
            )
        nc.sync.dma_start(w2_sb[0][:], w2_groups[0])
        with tc.tile_pool(name="stage", bufs=BLOCKS) as stage:
            x_f32 = [stage.tile([P, S], F32, name="x_f32") for k in range(BLOCKS)]
            for k in range(BLOCKS):
                nc.sync.dma_start(x_f32[k][:], x_blocks[:, k, :])
            for g in range(1, GROUPS):
                nc.sync.dma_start(w2_sb[g][:], w2_groups[g])
            for half in range(2):
                nc.sync.dma_start(w1_sb[half][:].rearrange("p (g j) o -> p g (j o)", j=2), w1_halves[half])
            for column, vector in ((g1, gamma1), (b1, beta1)):
                nc.scalar.dma_start(column[:], vector.rearrange("(p b) one -> p (b one)", b=BLOCKS))
            for k in range(BLOCKS):
                nc.vector.tensor_copy(x_bf[k][:], x_f32[k][:])

        nc.vector.memset(ones[:], 1.0)
        nc.vector.tensor_scalar_mul(b2_eighth[:], b2[:], 1.0 / NB)
        for a in range(BLOCKS):
            nc.vector.tensor_scalar_mul(gain[a][:], ones[:], g2[:, a : a + 1])

        y_bank = {}

        def y_pass(a, k):
            first = (k // BLOCKS) * BANK
            if k % BLOCKS == 0:
                y_bank[a] = banks.tile([P, BANK], F32, name="bank")
            nc.tensor.matmul(
                y_bank[a][:],
                w2_sb[a // 2][:, k % BLOCKS, a % 2 :: 2],
                x_bf[k % BLOCKS][:, first : first + BANK],
                start=(k % BLOCKS == 0),
                stop=(k % BLOCKS == BLOCKS - 1),
            )
            if k % BLOCKS == BLOCKS - 1:
                if a == 0 and first > 0:
                    nc.vector.tensor_copy(y[a][:, first : first + BANK], y_bank[a][:])
                else:
                    nc.scalar.copy(y[a][:, first : first + BANK], y_bank[a][:])

        with (
            tc.tile_pool(name="work", bufs=3) as work,
            tc.tile_pool(name="partial_sums", bufs=1) as partial_sums,
            tc.tile_pool(name="pairs", bufs=2) as pairs,
            tc.tile_pool(name="pooled", bufs=BLOCKS) as pooled,
            tc.tile_pool(name="results", bufs=BLOCKS) as results,
        ):
            scaled, h_eighth, h_bf, total, mn_turned, back, mn, mx, out_bank = {}, {}, {}, {}, {}, {}, {}, {}, {}

            def gather(u):
                c, a = divmod(u, BLOCKS)
                scaled[u] = work.tile([P, UNIT], F32, name="scaled")
                for first in range(0, UNIT, PIECE):
                    column = (c * UNIT + first) // 16
                    nc.vector.tensor_tensor(
                        scaled[u][:, first : first + PIECE],
                        y[a][:].indirect(offsets[:, column : column + PIECE // 16]),
                        gain[a][:],
                        ALU.mult,
                    )

            def rectify(u):
                a = u % BLOCKS
                h_eighth[u] = work.tile([P, CHUNK, NB], F32, name="h_eighth")
                nc.scalar.activation(
                    h_eighth[u][:].rearrange("p n t -> p (n t)"),
                    scaled[u][:],
                    ACT.Relu,
                    bias=b2_eighth[:, a : a + 1],
                    scale=1.0 / NB,
                )
                if u % 2 == 0:
                    h_bf[u // 2] = pairs.tile([P, 2 * CHUNK, NB], BF16, name="h_bf")
                nc.scalar.activation(
                    h_bf[u // 2][:, (u % 2) * CHUNK : (u % 2 + 1) * CHUNK, :].rearrange("p n t -> p (n t)"),
                    scaled[u][:],
                    ACT.Relu,
                    bias=b2[:, a : a + 1],
                    scale=1.0,
                )

            def sum_pass(u, k):
                first, t = (k // NB) * P, k % NB
                if k == 0:
                    total[u] = banks.tile([P, CHUNK], F32, name="total", tag="bank")
                nc.tensor.matmul(
                    total[u][:, first : first + P],
                    h_eighth[u][:, first : first + P, t],
                    identity[:],
                    is_transpose=True,
                    start=(t == 0),
                    stop=(t == NB - 1),
                )

            def maximum(u):
                pair = u // 2
                best4 = pairs.tile([P, 2 * CHUNK, 4], BF16, name="best4")
                nc.vector.tensor_tensor(best4[:], h_bf[pair][:, :, 0:4], h_bf[pair][:, :, 4:8], ALU.max)
                best2 = pairs.tile([P, 2 * CHUNK, 2], BF16, name="best2")
                nc.vector.tensor_tensor(best2[:], best4[:, :, 0:2], best4[:, :, 2:4], ALU.max)
                mx[pair] = pooled.tile([P, 2 * CHUNK], BF16, name="mx", bufs=BLOCKS // 2)
                nc.vector.tensor_tensor(mx[pair][:], best2[:, :, 0], best2[:, :, 1], ALU.max)

            def vector_sum(u):
                sum4 = partial_sums.tile([P, CHUNK, 4], F32, name="sum4")
                nc.vector.tensor_tensor(sum4[:], h_eighth[u][:, :, 0:4], h_eighth[u][:, :, 4:8], ALU.add)
                sum2 = partial_sums.tile([P, CHUNK, 2], F32, name="sum2")
                nc.vector.tensor_tensor(sum2[:], sum4[:, :, 0:2], sum4[:, :, 2:4], ALU.add)
                mn[u] = pooled.tile([P, CHUNK], BF16, name="mn")
                nc.vector.tensor_tensor(mn[u][:], sum2[:, :, 0], sum2[:, :, 1], ALU.add)

            def round_mean(u):
                mn_turned[u] = work.tile([P, CHUNK], BF16, name="mn_turned")
                nc.scalar.copy(mn_turned[u][:], total[u][:])

            def turn_back(u):
                back[u] = banks.tile([P, CHUNK], BF16, name="back", tag="bank")
                for first in range(0, CHUNK, P):
                    nc.tensor.transpose(
                        back[u][:, first : first + P], mn_turned[u][:, first : first + P], identity_bf[:]
                    )

            def fetch_mean(u):
                mn[u] = pooled.tile([P, CHUNK], BF16, name="mn")
                nc.scalar.copy(mn[u][:], back[u][:])

            def project_pass(u, k):
                c, a = divmod(u, BLOCKS)
                first_half, b = k < BLOCKS, k % BLOCKS
                if a == 0 and k == 0:
                    out_bank[c] = [out_banks.tile([P, BANK], F32, name="out_bank") for pair in range(OUT_BANKS)]
                side = (b % 2) * CHUNK
                nc.tensor.matmul(
                    out_bank[c][b // 2][:, side : side + CHUNK],
                    w1_sb[0 if first_half else 1][:, a, b::BLOCKS],
                    mx[u // 2][:, (u % 2) * CHUNK : (u % 2 + 1) * CHUNK] if first_half else mn[u][:],
                    start=(a == 0 and first_half and b % 2 == 0),
                    stop=(a == BLOCKS - 1 and not first_half and b % 2 == 1),
                )
                if a == BLOCKS - 1 and k == PASSES - 1:
                    store(c)

            def store(c):
                for b in range(BLOCKS):
                    side = (b % 2) * CHUNK
                    result = results.tile([P, CHUNK], F32, name="result")
                    if c == S // CHUNK - 1 and (b // 2) % 2 == 1:
                        nc.vector.tensor_scalar(
                            result[:],
                            out_bank[c][b // 2][:, side : side + CHUNK],
                            g1[:, b : b + 1],
                            b1[:, b : b + 1],
                            ALU.mult,
                            ALU.add,
                        )
                    else:
                        nc.scalar.activation(
                            result[:],
                            out_bank[c][b // 2][:, side : side + CHUNK],
                            ACT.Identity,
                            bias=b1[:, b : b + 1],
                            scale=g1[:, b : b + 1],
                        )
                    nc.sync.dma_start(out_blocks[:, b, c * CHUNK : (c + 1) * CHUNK], result[:])

            Y_AHEAD = 2
            SUM_LAG, PROJECT_LAG = 2, 5
            every_unit = range(UNITS)
            odd_units = range(1, UNITS, 2)
            vector_sums = [u for u in every_unit if u < VECTOR_SUMS or u == UNITS - 2]
            tensor_sums = [u for u in every_unit if u not in vector_sums]
            stages = (
                (round_mean, 3, tensor_sums),
                (turn_back, 3, tensor_sums),
                (vector_sum, SUM_LAG, vector_sums),
                (maximum, 2, odd_units),
                (rectify, 1, every_unit),
                (fetch_mean, 4, tensor_sums),
                (gather, 0, every_unit),
            )
            for a in range(Y_AHEAD):
                for k in range(PASSES):
                    y_pass(a, k)
            for step in range(UNITS + PROJECT_LAG):
                for k in range(PASSES):
                    if step + Y_AHEAD < BLOCKS:
                        y_pass(step + Y_AHEAD, k)
                for k in range(PASSES):
                    if step - SUM_LAG in tensor_sums:
                        sum_pass(step - SUM_LAG, k)
                for k in range(PASSES):
                    if step - PROJECT_LAG in every_unit:
                        project_pass(step - PROJECT_LAG, k)
                for run_stage, lag, its_units in stages:
                    if step - lag in its_units:
                        run_stage(step - lag)
